import numpy as np
import ml_dtypes


def mxq(x, axis, fmt="e4m3"):
    dtype, down = {"e4m3": (ml_dtypes.float8_e4m3fn, 7), "e5m2": (ml_dtypes.float8_e5m2, 14)}[fmt]
    v = np.moveaxis(np.asarray(x, np.float32).astype(ml_dtypes.bfloat16).astype(np.float64), axis, -1)
    blocks = v.reshape(v.shape[:-1] + (-1, 32))
    amax = np.abs(blocks).max(-1, keepdims=True)
    byte = np.maximum(np.where(amax > 0, np.frexp(amax)[1] - 1 + 127, 0) - down, 1)
    scale = np.exp2(byte - 127.0)
    codes = (blocks / scale).astype(np.float32).astype(dtype).astype(np.float64)
    return np.moveaxis((codes * scale).reshape(v.shape), -1, axis)


WIDE = False


def mx_kscale(k):
    if not WIDE:
        return np.ones(k)
    levels = np.array([10, -10, 5, -5, 0])
    a = np.random.permutation(np.resize(levels, k // 512 * 4)).reshape(k // 512, 4)
    idx = np.arange(k)
    return np.exp2(a[idx // 512, idx % 128 // 32])


BF16 = ml_dtypes.bfloat16


def bf(x):
    return np.asarray(x, np.float32).astype(BF16)


def f64(x):
    return np.asarray(x).astype(np.float64)


TOKENS, IN_FEATURES, OUT_FEATURES = 16384, 512, 128


def setup_inputs():
    a = np.sqrt(6.0 / (IN_FEATURES + OUT_FEATURES))
    s = mx_kscale(IN_FEATURES)
    return {"input": bf(np.random.standard_normal((TOKENS, IN_FEATURES)) * 4.0 / np.sqrt(IN_FEATURES) * (s / s.min())[None, :]),
            "weight": bf(np.random.uniform(-a, a, (OUT_FEATURES, IN_FEATURES)) / (s ** 4)[None, :])}


def reference(input, weight):
    w = f64(weight)
    abs_w = np.abs(w)
    abs_mean = np.mean(abs_w)
    w_ternary = np.where(abs_w > abs_mean, np.sign(w), np.zeros_like(w))
    return mxq(f64(input), 1, "e4m3") @ mxq(w_ternary, 1, "e4m3").T

@@ -1,0 +1,171 @@
+from contextlib import ExitStack
+
+import concourse.mybir as mybir
+from concourse.masks import make_identity
+
+F32 = mybir.dt.float32
+BF16 = mybir.dt.bfloat16
+U32 = mybir.dt.uint32
+U8 = mybir.dt.uint8
+FP8X4 = mybir.dt.float8_e4m3fn_x4
+ALU = mybir.AluOpType
+ACT = mybir.ActivationFunctionType
+
+P = 128
+TOKENS = 16384
+K = 512
+O = 128
+FLOPS = 2 * TOKENS * K * O
+
+SLOTS = TOKENS // P
+GROUP = 4
+NG = SLOTS // GROUP
+KW = K // 2
+
+PIN = True
+BUNCH = 2
+LAG = 2
+LOAD_SLOTS = (4, 4, 8, 16, 16, 16, 16, 16, 16, 16)
+STORE_SLOTS = (16, 16, 16, 16, 16, 16, 16, 16)
+XT_BANKS = 6
+PO_BANKS = 2
+G_BUFS = 3
+C_BUFS = 6
+
+
+def tile_ternarylinear_t_kernel(tc, x, weight, out):
+    nc = tc.nc
+    assert sum(LOAD_SLOTS) == SLOTS and sum(STORE_SLOTS) == SLOTS
+    xv = x.rearrange("(p t) k -> p (t k)", t=SLOTS)
+    ov = out.rearrange("(p t) o -> p (t o)", t=SLOTS)
+
+    with ExitStack() as ctx:
+        const = ctx.enter_context(tc.tile_pool(name="const", bufs=1))
+        xpool = ctx.enter_context(tc.tile_pool(name="xpool", bufs=1))
+        opool = ctx.enter_context(tc.tile_pool(name="opool", bufs=1))
+        gpool = ctx.enter_context(tc.tile_pool(name="gpool", bufs=G_BUFS))
+        cpool = ctx.enter_context(tc.tile_pool(name="cpool", bufs=C_BUFS))
+        psx = ctx.enter_context(tc.psum_pool(name="psx", bufs=XT_BANKS))
+        pso = ctx.enter_context(tc.psum_pool(name="pso", bufs=PO_BANKS))
+        if PIN:
+            ctx.enter_context(tc.manual_schedule())
+
+        w_sb = const.tile([P, K], BF16, name="w_sb")
+        nc.sync.dma_start(out=w_sb[:], in_=weight)
+        src = []
+        t0 = 0
+        for i, n in enumerate(LOAD_SLOTS):
+            xt = xpool.tile([P, n * K], BF16, name="x%d" % i)
+            nc.sync.dma_start(out=xt[:], in_=xv[:, t0 * K:(t0 + n) * K])
+            for a in range(0, n, GROUP):
+                src.append((xt[:].bitcast(F32), a * KW))
+            t0 += n
+        dst = []
+        stores = []
+        t0 = 0
+        for i, n in enumerate(STORE_SLOTS):
+            ot = opool.tile([P, n * O], F32, name="o%d" % i)
+            stores.append((ot, t0, n))
+            for a in range(0, n, GROUP):
+                dst.append((i, ot, a * O, a + GROUP == n))
+            t0 += n
+
+        ident = const.tile([P, P], F32, name="ident")
+        make_identity(nc, ident[:])
+        ones = const.tile([P, P], F32, name="ones")
+        nc.vector.memset(ones[:], 1.0 / (O * K))
+
+        absw = const.tile([P, K], BF16, name="absw")
+        rowsum = const.tile([P, 1], F32, name="rowsum")
+        nc.scalar.activation(out=absw[:], in_=w_sb[:], func=ACT.Abs, accum_out=rowsum[:])
+        wps = psx.tile([P, 512], F32, name="wps", tag="xt")
+        ww = w_sb[:].bitcast(F32)
+        for u in range(2):
+            nc.tensor.transpose(wps[:, u * P:(u + 1) * P], ww[:, u * P:(u + 1) * P], ident[:])
+        wg = const.tile([P, K], BF16, name="wg")
+        nc.vector.tensor_copy(
+            out=wg[:].bitcast(F32).rearrange("p (r u) -> p r u", u=2),
+            in_=wps[:, 0:2 * P].rearrange("p (u r) -> p r u", u=2),
+        )
+        tot = pso.tile([P, 512], F32, name="tot", tag="po")
+        nc.tensor.matmul(out=tot[:, 0:1], lhsT=ones[:], rhs=rowsum[:], start=True, stop=True)
+        mean = const.tile([P, 1], F32, name="mean")
+        nc.vector.tensor_copy(out=mean[:], in_=tot[:, 0:1])
+        neg = const.tile([P, K], BF16, name="neg")
+        nc.vector.tensor_scalar(out=neg[:], in0=wg[:], scalar1=-1.0, scalar2=mean[:, 0:1],
+                                op0=ALU.mult, op1=ALU.is_gt)
+        tern = const.tile([P, K], BF16, name="tern", align_bytes=64)
+        nc.vector.scalar_tensor_tensor(out=tern[:], in0=wg[:], scalar=mean[:, 0:1], in1=neg[:],
+                                       op0=ALU.is_gt, op1=ALU.subtract)
+        t_codes = const.tile([P, O], U32, name="t_codes", align_bytes=64)
+        t_scales = const.tile([P, O], U8, name="t_scales", align_bytes=64)
+        nc.vector.quantize_mx(out=t_codes[:].bitcast(FP8X4), scales=t_scales[:], in_=tern[:])
+
+        banks = {}
+        grouped = {}
+        quantised = {}
+        results = {}
+
+        def transposes(g):
+            xw, w0 = src[g]
+            pair = []
+            for h in range(2):
+                bank = psx.tile([P, 512], F32, name="bank", tag="xt")
+                for j in range(4):
+                    c = w0 + (2 * h) * KW + j * P
+                    nc.tensor.transpose(bank[:, j * P:(j + 1) * P], xw[:, c:c + P], ident[:])
+                pair.append(bank)
+            banks[g] = pair
+
+        def copies(g):
+            gt = gpool.tile([P, GROUP * P * 4], BF16, name="gt", tag="gt", align_bytes=64)
+            gw = gt[:].bitcast(F32).rearrange("p (s r u) -> p s r u", s=GROUP, u=2)
+            a, b = banks[g]
+            nc.vector.tensor_copy(out=gw[:, 0:2], in_=a[:].rearrange("p (s u r) -> p s r u", s=2, u=2))
+            nc.scalar.copy(out=gw[:, 2:4], in_=b[:].rearrange("p (s u r) -> p s r u", s=2, u=2))
+            grouped[g] = gt
+
+        def quantise(g):
+            codes = cpool.tile([P, GROUP * P], U32, name="codes", tag="codes", align_bytes=64)
+            scales = cpool.tile([P, GROUP * P], U8, name="scales", tag="scales", align_bytes=64)
+            nc.vector.quantize_mx(out=codes[:].bitcast(FP8X4), scales=scales[:], in_=grouped[g][:])
+            quantised[g] = (codes, scales)
+
+        def multiply(g):
+            codes, scales = quantised[g]
+            po = pso.tile([P, 512], F32, name="po", tag="po")
+            for s in range(GROUP):
+                nc.tensor.matmul_mx(
+                    out=po[:, s * O:(s + 1) * O],
+                    lhsT=codes[:, s * P:(s + 1) * P].bitcast(FP8X4),
+                    lhsT_scale=scales[:, s * P:(s + 1) * P],
+                    rhs=t_codes[:].bitcast(FP8X4),
+                    rhs_scale=t_scales[:],
+                    start=True,
+                    stop=True,
+                )
+            results[g] = po
+
+        def leave(g):
+            i, ot, c0, last = dst[g]
+            nc.scalar.copy(out=ot[:, c0:c0 + GROUP * O], in_=results[g][:])
+            if last:
+                ot, t0, n = stores[i]
+                nc.sync.dma_start(out=ov[:, t0 * O:(t0 + n) * O], in_=ot[:])
+
+        nb = NG // BUNCH
+        for j in range(nb + LAG):
+            mine = [g for g in range(j * BUNCH, (j + 1) * BUNCH) if g < NG]
+            for g in mine:
+                transposes(g)
+            for g in mine:
+                copies(g)
+                if g >= 1:
+                    quantise(g - 1)
+            if j == nb:
+                quantise(NG - 1)
+            late = [g for g in range((j - LAG) * BUNCH, (j - LAG + 1) * BUNCH) if 0 <= g < NG]
+            for g in late:
+                multiply(g)
+            for g in late:
+                leave(g)

@@ -26,7 +26,7 @@ PIN = True
 BUNCH = 2
 LAG = 2
 LOAD_SLOTS = (4, 4, 8, 16, 16, 16, 16, 16, 16, 16)
-STORE_SLOTS = (16, 16, 16, 16, 16, 16, 16, 16)
+STORE_SLOTS = (64, 32, 16, 16)
 XT_BANKS = 6
 PO_BANKS = 2
 G_BUFS = 3

@@ -22,7 +22,7 @@ GROUP = 4
 NG = SLOTS // GROUP
 KW = K // 2
 
-PIN = True
+PIN = False
 BUNCH = 2
 LAG = 2
 LOAD_SLOTS = (4, 4, 8, 16, 16, 16, 16, 16, 16, 16)

@@ -25,8 +25,7 @@ KW = K // 2
 PIN = False
 BUNCH = 2
 LAG = 2
-LOAD_SLOTS = (4, 4, 8, 16, 16, 16, 16, 16, 16, 16)
-STORE_SLOTS = (64, 32, 16, 16)
+REGIONS = ((40, (4, 12, 24)), (40, (20, 20)), (24, (24,)), (24, (24,)))
 XT_BANKS = 6
 PO_BANKS = 2
 G_BUFS = 3
@@ -35,9 +34,8 @@ C_BUFS = 6
 
 def tile_ternarylinear_t_kernel(tc, x, weight, out):
     nc = tc.nc
-    assert sum(LOAD_SLOTS) == SLOTS and sum(STORE_SLOTS) == SLOTS
-    xv = x.rearrange("(p t) k -> p (t k)", t=SLOTS)
-    ov = out.rearrange("(p t) o -> p (t o)", t=SLOTS)
+    assert sum(n for n, loads in REGIONS) == SLOTS
+    assert all(sum(loads) == n for n, loads in REGIONS)
 
     with ExitStack() as ctx:
         const = ctx.enter_context(tc.tile_pool(name="const", bufs=1))
@@ -53,22 +51,26 @@ def tile_ternarylinear_t_kernel(tc, x, weight, out):
         w_sb = const.tile([P, K], BF16, name="w_sb")
         nc.sync.dma_start(out=w_sb[:], in_=weight)
         src = []
-        t0 = 0
-        for i, n in enumerate(LOAD_SLOTS):
-            xt = xpool.tile([P, n * K], BF16, name="x%d" % i)
-            nc.sync.dma_start(out=xt[:], in_=xv[:, t0 * K:(t0 + n) * K])
-            for a in range(0, n, GROUP):
-                src.append((xt[:].bitcast(F32), a * KW))
-            t0 += n
+        r0 = 0
+        for r, (size, loads) in enumerate(REGIONS):
+            xv = x[r0 * P:(r0 + size) * P, :].rearrange("(p t) k -> p (t k)", t=size)
+            t0 = 0
+            for i, n in enumerate(loads):
+                xt = xpool.tile([P, n * K], BF16, name="x%d_%d" % (r, i))
+                nc.sync.dma_start(out=xt[:], in_=xv[:, t0 * K:(t0 + n) * K])
+                for a in range(0, n, GROUP):
+                    src.append((xt[:].bitcast(F32), a * KW))
+                t0 += n
+            r0 += size
         dst = []
         stores = []
-        t0 = 0
-        for i, n in enumerate(STORE_SLOTS):
+        r0 = 0
+        for i, (n, loads) in enumerate(REGIONS):
             ot = opool.tile([P, n * O], F32, name="o%d" % i)
-            stores.append((ot, t0, n))
+            stores.append((ot, out[r0 * P:(r0 + n) * P, :].rearrange("(p t) o -> p (t o)", t=n)))
             for a in range(0, n, GROUP):
                 dst.append((i, ot, a * O, a + GROUP == n))
-            t0 += n
+            r0 += n
 
         ident = const.tile([P, P], F32, name="ident")
         make_identity(nc, ident[:])
@@ -150,8 +152,8 @@ def tile_ternarylinear_t_kernel(tc, x, weight, out):
             i, ot, c0, last = dst[g]
             nc.scalar.copy(out=ot[:, c0:c0 + GROUP * O], in_=results[g][:])
             if last:
-                ot, t0, n = stores[i]
-                nc.sync.dma_start(out=ov[:, t0 * O:(t0 + n) * O], in_=ot[:])
+                ot, rows = stores[i]
+                nc.sync.dma_start(out=rows, in_=ot[:])
 
         nb = NG // BUNCH
         for j in range(nb + LAG):

@@ -25,7 +25,7 @@ KW = K // 2
 PIN = False
 BUNCH = 2
 LAG = 2
-REGIONS = ((40, (4, 12, 24)), (40, (20, 20)), (24, (24,)), (24, (24,)))
+REGIONS = ((40, (4, 8, 12, 16)), (40, (20, 20)), (24, (24,)), (24, (24,)))
 XT_BANKS = 6
 PO_BANKS = 2
 G_BUFS = 3

@@ -49,7 +49,7 @@ def tile_ternarylinear_t_kernel(tc, x, weight, out):
             ctx.enter_context(tc.manual_schedule())
 
         w_sb = const.tile([P, K], BF16, name="w_sb")
-        nc.sync.dma_start(out=w_sb[:], in_=weight)
+        nc.scalar.dma_start(out=w_sb[:], in_=weight)
         src = []
         r0 = 0
         for r, (size, loads) in enumerate(REGIONS):

from contextlib import ExitStack

import concourse.mybir as mybir
from concourse.masks import make_identity

F32 = mybir.dt.float32
BF16 = mybir.dt.bfloat16
U32 = mybir.dt.uint32
U8 = mybir.dt.uint8
FP8X4 = mybir.dt.float8_e4m3fn_x4
ALU = mybir.AluOpType
ACT = mybir.ActivationFunctionType

P = 128
TOKENS = 16384
K = 512
O = 128
FLOPS = 2 * TOKENS * K * O

SLOTS = TOKENS // P
GROUP = 4
NG = SLOTS // GROUP
KW = K // 2

PIN = False
BUNCH = 2
LAG = 2
REGIONS = ((40, (4, 8, 12, 16)), (40, (20, 20)), (24, (24,)), (24, (24,)))
XT_BANKS = 6
PO_BANKS = 2
G_BUFS = 3
C_BUFS = 6


def tile_ternarylinear_t_kernel(tc, x, weight, out):
    nc = tc.nc
    assert sum(n for n, loads in REGIONS) == SLOTS
    assert all(sum(loads) == n for n, loads in REGIONS)

    with ExitStack() as ctx:
        const = ctx.enter_context(tc.tile_pool(name="const", bufs=1))
        xpool = ctx.enter_context(tc.tile_pool(name="xpool", bufs=1))
        opool = ctx.enter_context(tc.tile_pool(name="opool", bufs=1))
        gpool = ctx.enter_context(tc.tile_pool(name="gpool", bufs=G_BUFS))
        cpool = ctx.enter_context(tc.tile_pool(name="cpool", bufs=C_BUFS))
        psx = ctx.enter_context(tc.psum_pool(name="psx", bufs=XT_BANKS))
        pso = ctx.enter_context(tc.psum_pool(name="pso", bufs=PO_BANKS))
        if PIN:
            ctx.enter_context(tc.manual_schedule())

        w_sb = const.tile([P, K], BF16, name="w_sb")
        nc.scalar.dma_start(out=w_sb[:], in_=weight)
        src = []
        r0 = 0
        for r, (size, loads) in enumerate(REGIONS):
            xv = x[r0 * P:(r0 + size) * P, :].rearrange("(p t) k -> p (t k)", t=size)
            t0 = 0
            for i, n in enumerate(loads):
                xt = xpool.tile([P, n * K], BF16, name="x%d_%d" % (r, i))
                nc.sync.dma_start(out=xt[:], in_=xv[:, t0 * K:(t0 + n) * K])
                for a in range(0, n, GROUP):
                    src.append((xt[:].bitcast(F32), a * KW))
                t0 += n
            r0 += size
        dst = []
        stores = []
        r0 = 0
        for i, (n, loads) in enumerate(REGIONS):
            ot = opool.tile([P, n * O], F32, name="o%d" % i)
            stores.append((ot, out[r0 * P:(r0 + n) * P, :].rearrange("(p t) o -> p (t o)", t=n)))
            for a in range(0, n, GROUP):
                dst.append((i, ot, a * O, a + GROUP == n))
            r0 += n

        ident = const.tile([P, P], F32, name="ident")
        make_identity(nc, ident[:])
        ones = const.tile([P, P], F32, name="ones")
        nc.vector.memset(ones[:], 1.0 / (O * K))

        absw = const.tile([P, K], BF16, name="absw")
        rowsum = const.tile([P, 1], F32, name="rowsum")
        nc.scalar.activation(out=absw[:], in_=w_sb[:], func=ACT.Abs, accum_out=rowsum[:])
        wps = psx.tile([P, 512], F32, name="wps", tag="xt")
        ww = w_sb[:].bitcast(F32)
        for u in range(2):
            nc.tensor.transpose(wps[:, u * P:(u + 1) * P], ww[:, u * P:(u + 1) * P], ident[:])
        wg = const.tile([P, K], BF16, name="wg")
        nc.vector.tensor_copy(
            out=wg[:].bitcast(F32).rearrange("p (r u) -> p r u", u=2),
            in_=wps[:, 0:2 * P].rearrange("p (u r) -> p r u", u=2),
        )
        tot = pso.tile([P, 512], F32, name="tot", tag="po")
        nc.tensor.matmul(out=tot[:, 0:1], lhsT=ones[:], rhs=rowsum[:], start=True, stop=True)
        mean = const.tile([P, 1], F32, name="mean")
        nc.vector.tensor_copy(out=mean[:], in_=tot[:, 0:1])
        neg = const.tile([P, K], BF16, name="neg")
        nc.vector.tensor_scalar(out=neg[:], in0=wg[:], scalar1=-1.0, scalar2=mean[:, 0:1],
                                op0=ALU.mult, op1=ALU.is_gt)
        tern = const.tile([P, K], BF16, name="tern", align_bytes=64)
        nc.vector.scalar_tensor_tensor(out=tern[:], in0=wg[:], scalar=mean[:, 0:1], in1=neg[:],
                                       op0=ALU.is_gt, op1=ALU.subtract)
        t_codes = const.tile([P, O], U32, name="t_codes", align_bytes=64)
        t_scales = const.tile([P, O], U8, name="t_scales", align_bytes=64)
        nc.vector.quantize_mx(out=t_codes[:].bitcast(FP8X4), scales=t_scales[:], in_=tern[:])

        banks = {}
        grouped = {}
        quantised = {}
        results = {}

        def transposes(g):
            xw, w0 = src[g]
            pair = []
            for h in range(2):
                bank = psx.tile([P, 512], F32, name="bank", tag="xt")
                for j in range(4):
                    c = w0 + (2 * h) * KW + j * P
                    nc.tensor.transpose(bank[:, j * P:(j + 1) * P], xw[:, c:c + P], ident[:])
                pair.append(bank)
            banks[g] = pair

        def copies(g):
            gt = gpool.tile([P, GROUP * P * 4], BF16, name="gt", tag="gt", align_bytes=64)
            gw = gt[:].bitcast(F32).rearrange("p (s r u) -> p s r u", s=GROUP, u=2)
            a, b = banks[g]
            nc.vector.tensor_copy(out=gw[:, 0:2], in_=a[:].rearrange("p (s u r) -> p s r u", s=2, u=2))
            nc.scalar.copy(out=gw[:, 2:4], in_=b[:].rearrange("p (s u r) -> p s r u", s=2, u=2))
            grouped[g] = gt

        def quantise(g):
            codes = cpool.tile([P, GROUP * P], U32, name="codes", tag="codes", align_bytes=64)
            scales = cpool.tile([P, GROUP * P], U8, name="scales", tag="scales", align_bytes=64)
            nc.vector.quantize_mx(out=codes[:].bitcast(FP8X4), scales=scales[:], in_=grouped[g][:])
            quantised[g] = (codes, scales)

        def multiply(g):
            codes, scales = quantised[g]
            po = pso.tile([P, 512], F32, name="po", tag="po")
            for s in range(GROUP):
                nc.tensor.matmul_mx(
                    out=po[:, s * O:(s + 1) * O],
                    lhsT=codes[:, s * P:(s + 1) * P].bitcast(FP8X4),
                    lhsT_scale=scales[:, s * P:(s + 1) * P],
                    rhs=t_codes[:].bitcast(FP8X4),
                    rhs_scale=t_scales[:],
                    start=True,
                    stop=True,
                )
            results[g] = po

        def leave(g):
            i, ot, c0, last = dst[g]
            nc.scalar.copy(out=ot[:, c0:c0 + GROUP * O], in_=results[g][:])
            if last:
                ot, rows = stores[i]
                nc.sync.dma_start(out=rows, in_=ot[:])

        nb = NG // BUNCH
        for j in range(nb + LAG):
            mine = [g for g in range(j * BUNCH, (j + 1) * BUNCH) if g < NG]
            for g in mine:
                transposes(g)
            for g in mine:
                copies(g)
                if g >= 1:
                    quantise(g - 1)
            if j == nb:
                quantise(NG - 1)
            late = [g for g in range((j - LAG) * BUNCH, (j - LAG + 1) * BUNCH) if 0 <= g < NG]
            for g in late:
                multiply(g)
            for g in late:
                leave(g)
